import numpy as np
import ml_dtypes


def mxq(x, axis, fmt="e4m3"):
    dtype, down = {"e4m3": (ml_dtypes.float8_e4m3fn, 7), "e5m2": (ml_dtypes.float8_e5m2, 14)}[fmt]
    v = np.moveaxis(np.asarray(x, np.float32).astype(ml_dtypes.bfloat16).astype(np.float64), axis, -1)
    blocks = v.reshape(v.shape[:-1] + (-1, 32))
    amax = np.abs(blocks).max(-1, keepdims=True)
    byte = np.maximum(np.where(amax > 0, np.frexp(amax)[1] - 1 + 127, 0) - down, 1)
    scale = np.exp2(byte - 127.0)
    codes = (blocks / scale).astype(np.float32).astype(dtype).astype(np.float64)
    return np.moveaxis((codes * scale).reshape(v.shape), -1, axis)


WIDE = False


def mx_kscale(k):
    if not WIDE:
        return np.ones(k)
    levels = np.array([20, -20, 10, -10, 0])
    a = np.random.permutation(np.resize(levels, k // 512 * 4)).reshape(k // 512, 4)
    idx = np.arange(k)
    return np.exp2(a[idx // 512, idx % 128 // 32])


BF16 = ml_dtypes.bfloat16


def bf(x):
    return np.asarray(x, np.float32).astype(BF16)


def f64(x):
    return np.asarray(x).astype(np.float64)


B, S, D_IN, D_OUT = 3, 512, 1024, 1024


def relative_shift(x):
    b, s, d = x.shape
    padded = np.concatenate([np.zeros((b, 1, d)), x], axis=1).reshape(s + 1, b, d)
    return padded[1:].reshape(b, s, d)


def relative_shift_adjoint(g, b, s):
    d = g.shape[1]
    padded = np.concatenate([np.zeros((b, d)), g], axis=0).reshape(b, s + 1, d)
    return padded[:, 1:]


def setup_inputs():
    u = mx_kscale(D_OUT)
    pos_embed = np.random.standard_normal((B, S, D_IN))
    W_r = np.random.standard_normal((D_OUT, D_IN)) * 1.2 / np.sqrt(D_IN) / u[:, None]
    b_r = np.random.standard_normal(D_OUT) * 0.3
    g = np.random.standard_normal((B, S, D_OUT)) * np.exp2(np.random.randint(-12, 1, (B, S, 1))) * 8.0 * u
    return {"pos_embed": bf(pos_embed), "W_r": bf(W_r), "b_r": bf(b_r), "grad_out": bf(g)}


def reference(pos_embed, W_r, b_r, grad_out):
    g = f64(grad_out).reshape(B * S, D_OUT)
    gs = mxq(g, 1, "e5m2") @ mxq(f64(W_r), 0, "e4m3")
    return relative_shift_adjoint(gs, B, S)

@@ -1,0 +1,162 @@
+from contextlib import ExitStack
+
+import concourse.mybir as mybir
+from concourse.masks import make_identity
+
+BF16 = mybir.dt.bfloat16
+F32 = mybir.dt.float32
+U32 = mybir.dt.uint32
+U8 = mybir.dt.uint8
+E4M3_X4 = mybir.dt.float8_e4m3fn_x4
+E5M2_X4 = mybir.dt.float8_e5m2_x4
+
+BATCH, SEQ, D_IN, D_OUT = 3, 512, 1024, 1024
+ROWS = BATCH * SEQ
+P = 128
+PACK = 4
+PASSES = D_OUT // (P * PACK)
+N_TILE = 512
+N_TILES = D_IN // N_TILE
+TILES_PER_BATCH = SEQ // P
+AHEAD = 2
+
+FLOPS = 2 * ROWS * D_OUT * D_IN
+BYTES = 2 * ROWS * D_OUT + 2 * D_OUT * D_IN + 4 * ROWS * D_IN
+
+
+def row_tiles():
+    tiles = []
+    for b in range(BATCH):
+        first_s = 2 if b == 0 else 0
+        for s in range(first_s, SEQ, P):
+            tiles.append(((SEQ + 1) * b + s - 2, SEQ * b + s, min(P, SEQ - s)))
+    return tiles
+
+
+def tile_relativemultiheadattention_pa_kernel(tc, pos_embed, W_r, b_r, grad_out, out):
+    nc = tc.nc
+    grad_rows = grad_out.flatten_outer_dims()
+    out_rows = out.flatten_outer_dims()
+    tiles = row_tiles()
+    n_tiles = len(tiles)
+    assert n_tiles == BATCH * TILES_PER_BATCH
+
+    with ExitStack() as ctx:
+        keep = ctx.enter_context(tc.tile_pool(name="keep", bufs=1))
+        per_tile = ctx.enter_context(tc.tile_pool(name="per_tile", bufs=n_tiles))
+        transposed = ctx.enter_context(tc.psum_pool(name="transposed", bufs=TILES_PER_BATCH))
+        sums = ctx.enter_context(tc.psum_pool(name="sums", bufs=4))
+
+        identity = keep.tile([P, P], F32)
+        make_identity(nc, identity[:])
+        zeros = keep.tile([2, D_IN], F32)
+        nc.vector.memset(zeros[:], 0.0)
+
+        w_raw = keep.tile([P, PASSES, PACK, D_IN], BF16)
+        w_view = W_r.rearrange("(g u p e) n -> g p u (e n)", g=PASSES, u=2, p=P, e=2)
+        for g in range(PASSES):
+            nc.sync.dma_start(out=w_raw[:, g].rearrange("p (u e) n -> p u (e n)", u=2), in_=w_view[g])
+
+        raw_tiles = []
+        for first_g, first_o, rows in tiles:
+            raw = per_tile.tile([P, D_OUT], BF16)
+            nc.sync.dma_start(out=raw[0:rows, :], in_=grad_rows[first_g : first_g + rows, :])
+            if rows < P:
+                assert P - rows == BATCH - 1
+                nc.sync.dma_start(out=raw[rows:P, :], in_=grad_rows[SEQ - 2 : ROWS - SEQ : SEQ + 1, :])
+            raw_tiles.append(raw)
+
+        nc.sync.dma_start(out=out_rows[0:2, :], in_=zeros[:])
+
+        w_grouped = keep.tile([P, PASSES, D_IN, PACK], BF16, align_bytes=64)
+        w_codes = keep.tile([P, PASSES, D_IN], U32, align_bytes=64)
+        w_scales = keep.tile([P, PASSES, D_IN], U8, align_bytes=64)
+
+        def regroup_w(g, n):
+            half = N_TILE // 2
+            shares = ((nc.vector.tensor_copy, n * N_TILE), (nc.scalar.copy, n * N_TILE + half))
+            for copy, first in shares:
+                cols = slice(first, first + half)
+                copy(
+                    out=w_grouped[:, g, cols, :].rearrange("p (c i) t -> p c t i", i=4),
+                    in_=w_raw[:, g, :, cols].rearrange("p t (c i) -> p c t i", i=4),
+                )
+
+        def quantise_w(g, n):
+            cols = slice(n * N_TILE, (n + 1) * N_TILE)
+            nc.vector.quantize_mx(
+                out=w_codes[:, g, cols].bitcast(E4M3_X4),
+                scales=w_scales[:, g, cols],
+                in_=w_grouped[:, g, cols, :].rearrange("p c t -> p (c t)"),
+            )
+
+        pieces = [(g, n) for g in range(PASSES) for n in range(N_TILES)]
+        for i, piece in enumerate(pieces):
+            regroup_w(*piece)
+            if i > 0:
+                quantise_w(*pieces[i - 1])
+        quantise_w(*pieces[-1])
+
+        g_codes = keep.tile([P, n_tiles, PASSES, P], U32, align_bytes=64)
+        g_scales = keep.tile([P, n_tiles, PASSES, P], U8, align_bytes=64)
+        banks = {}
+        grouped_tiles = {}
+
+        def transpose_batch(b):
+            for j in range(b * TILES_PER_BATCH, (b + 1) * TILES_PER_BATCH):
+                words = raw_tiles[j][:].bitcast(F32)
+                bank = transposed.tile([P, PASSES * 2, P], F32)
+                for c in range(PASSES * 2):
+                    nc.tensor.transpose(bank[:, c, :], words[:, c * P : (c + 1) * P], identity[:])
+                banks[j] = bank
+
+        def regroup_tile(j):
+            grouped = per_tile.tile([P, PASSES * P * PACK], BF16, align_bytes=64)
+            nc.scalar.copy(
+                out=grouped[:].bitcast(F32).rearrange("p (g r u) -> p g r u", g=PASSES, u=2),
+                in_=banks[j][:].rearrange("p (g u) r -> p g r u", u=2),
+            )
+            grouped_tiles[j] = grouped
+
+        def quantise_tile(j):
+            nc.vector.quantize_mx(
+                out=g_codes[:, j].rearrange("p g r -> p (g r)").bitcast(E5M2_X4),
+                scales=g_scales[:, j].rearrange("p g r -> p (g r)"),
+                in_=grouped_tiles[j][:],
+            )
+
+        def multiply_tile(j):
+            first_g, first_o, rows = tiles[j]
+            result = per_tile.tile([P, D_IN], F32)
+            for n in range(N_TILES):
+                cols = slice(n * N_TILE, (n + 1) * N_TILE)
+                acc = sums.tile([P, N_TILE], F32)
+                for g in range(PASSES):
+                    nc.tensor.matmul_mx(
+                        out=acc[:],
+                        lhsT=g_codes[:, j, g, :].bitcast(E5M2_X4),
+                        lhsT_scale=g_scales[:, j, g, :],
+                        rhs=w_codes[:, g, cols].bitcast(E4M3_X4),
+                        rhs_scale=w_scales[:, g, cols],
+                        start=(g == 0),
+                        stop=(g == PASSES - 1),
+                    )
+                if n % 2 == 0:
+                    nc.vector.tensor_copy(out=result[:, cols], in_=acc[:])
+                else:
+                    nc.scalar.copy(out=result[:, cols], in_=acc[:])
+            nc.sync.dma_start(out=out_rows[first_o : first_o + rows, :], in_=result[0:rows, :])
+
+        transpose_batch(0)
+        for j in range(AHEAD):
+            regroup_tile(j)
+            quantise_tile(j)
+        for j in range(n_tiles):
+            ahead = j + AHEAD
+            if ahead < n_tiles:
+                if ahead % TILES_PER_BATCH == 0:
+                    transpose_batch(ahead // TILES_PER_BATCH)
+                regroup_tile(ahead)
+            multiply_tile(j)
+            if ahead < n_tiles:
+                quantise_tile(ahead)

@@ -46,6 +46,7 @@ def tile_relativemultiheadattention_pa_kernel(tc, pos_embed, W_r, b_r, grad_out,
         per_tile = ctx.enter_context(tc.tile_pool(name="per_tile", bufs=n_tiles))
         transposed = ctx.enter_context(tc.psum_pool(name="transposed", bufs=TILES_PER_BATCH))
         sums = ctx.enter_context(tc.psum_pool(name="sums", bufs=4))
+        ctx.enter_context(tc.manual_schedule())
 
         identity = keep.tile([P, P], F32)
         make_identity(nc, identity[:])

@@ -17,8 +17,9 @@ PACK = 4
 PASSES = D_OUT // (P * PACK)
 N_TILE = 512
 N_TILES = D_IN // N_TILE
-TILES_PER_BATCH = SEQ // P
+RUN = 3
 AHEAD = 2
+PSUM_BANKS = 8
 
 FLOPS = 2 * ROWS * D_OUT * D_IN
 BYTES = 2 * ROWS * D_OUT + 2 * D_OUT * D_IN + 4 * ROWS * D_IN
@@ -39,13 +40,13 @@ def tile_relativemultiheadattention_pa_kernel(tc, pos_embed, W_r, b_r, grad_out,
     out_rows = out.flatten_outer_dims()
     tiles = row_tiles()
     n_tiles = len(tiles)
-    assert n_tiles == BATCH * TILES_PER_BATCH
+    assert n_tiles % RUN == 0 and AHEAD <= RUN
 
     with ExitStack() as ctx:
         keep = ctx.enter_context(tc.tile_pool(name="keep", bufs=1))
         per_tile = ctx.enter_context(tc.tile_pool(name="per_tile", bufs=n_tiles))
-        transposed = ctx.enter_context(tc.psum_pool(name="transposed", bufs=TILES_PER_BATCH))
-        sums = ctx.enter_context(tc.psum_pool(name="sums", bufs=4))
+        transposed = ctx.enter_context(tc.psum_pool(name="transposed", bufs=RUN))
+        sums = ctx.enter_context(tc.psum_pool(name="sums", bufs=PSUM_BANKS - RUN))
         ctx.enter_context(tc.manual_schedule())
 
         identity = keep.tile([P, P], F32)
@@ -55,18 +56,26 @@ def tile_relativemultiheadattention_pa_kernel(tc, pos_embed, W_r, b_r, grad_out,
 
         w_raw = keep.tile([P, PASSES, PACK, D_IN], BF16)
         w_view = W_r.rearrange("(g u p e) n -> g p u (e n)", g=PASSES, u=2, p=P, e=2)
-        for g in range(PASSES):
+
+        def load_w(g):
             nc.sync.dma_start(out=w_raw[:, g].rearrange("p (u e) n -> p u (e n)", u=2), in_=w_view[g])
 
-        raw_tiles = []
-        for first_g, first_o, rows in tiles:
+        raw_tiles = {}
+
+        def load_tile(j):
+            first_g, first_o, rows = tiles[j]
             raw = per_tile.tile([P, D_OUT], BF16)
             nc.sync.dma_start(out=raw[0:rows, :], in_=grad_rows[first_g : first_g + rows, :])
             if rows < P:
                 assert P - rows == BATCH - 1
                 nc.sync.dma_start(out=raw[rows:P, :], in_=grad_rows[SEQ - 2 : ROWS - SEQ : SEQ + 1, :])
-            raw_tiles.append(raw)
+            raw_tiles[j] = raw
 
+        load_w(0)
+        load_tile(0)
+        load_w(1)
+        for j in range(1, n_tiles):
+            load_tile(j)
         nc.sync.dma_start(out=out_rows[0:2, :], in_=zeros[:])
 
         w_grouped = keep.tile([P, PASSES, D_IN, PACK], BF16, align_bytes=64)
@@ -91,20 +100,13 @@ def tile_relativemultiheadattention_pa_kernel(tc, pos_embed, W_r, b_r, grad_out,
                 in_=w_grouped[:, g, cols, :].rearrange("p c t -> p (c t)"),
             )
 
-        pieces = [(g, n) for g in range(PASSES) for n in range(N_TILES)]
-        for i, piece in enumerate(pieces):
-            regroup_w(*piece)
-            if i > 0:
-                quantise_w(*pieces[i - 1])
-        quantise_w(*pieces[-1])
-
         g_codes = keep.tile([P, n_tiles, PASSES, P], U32, align_bytes=64)
         g_scales = keep.tile([P, n_tiles, PASSES, P], U8, align_bytes=64)
         banks = {}
         grouped_tiles = {}
 
-        def transpose_batch(b):
-            for j in range(b * TILES_PER_BATCH, (b + 1) * TILES_PER_BATCH):
+        def transpose_tiles(first, end):
+            for j in range(first, end):
                 words = raw_tiles[j][:].bitcast(F32)
                 bank = transposed.tile([P, PASSES * 2, P], F32)
                 for c in range(PASSES * 2):
@@ -146,17 +148,26 @@ def tile_relativemultiheadattention_pa_kernel(tc, pos_embed, W_r, b_r, grad_out,
                     nc.vector.tensor_copy(out=result[:, cols], in_=acc[:])
                 else:
                     nc.scalar.copy(out=result[:, cols], in_=acc[:])
-            nc.sync.dma_start(out=out_rows[first_o : first_o + rows, :], in_=result[0:rows, :])
+                nc.sync.dma_start(out=out_rows[first_o : first_o + rows, cols], in_=result[0:rows, cols])
 
-        transpose_batch(0)
-        for j in range(AHEAD):
+        for g in range(PASSES):
+            for n in range(N_TILES):
+                regroup_w(g, n)
+            for n in range(N_TILES):
+                quantise_w(g, n)
+            if g == 0:
+                transpose_tiles(0, 1)
+                regroup_tile(0)
+                quantise_tile(0)
+        transpose_tiles(1, RUN)
+        for j in range(1, AHEAD):
             regroup_tile(j)
             quantise_tile(j)
         for j in range(n_tiles):
             ahead = j + AHEAD
             if ahead < n_tiles:
-                if ahead % TILES_PER_BATCH == 0:
-                    transpose_batch(ahead // TILES_PER_BATCH)
+                if ahead % RUN == 0:
+                    transpose_tiles(ahead, ahead + RUN)
                 regroup_tile(ahead)
             multiply_tile(j)
             if ahead < n_tiles:

@@ -20,6 +20,7 @@ N_TILES = D_IN // N_TILE
 RUN = 3
 AHEAD = 2
 PSUM_BANKS = 8
+WARM = 6
 
 FLOPS = 2 * ROWS * D_OUT * D_IN
 BYTES = 2 * ROWS * D_OUT + 2 * D_OUT * D_IN + 4 * ROWS * D_IN
@@ -53,6 +54,8 @@ def tile_relativemultiheadattention_pa_kernel(tc, pos_embed, W_r, b_r, grad_out,
         make_identity(nc, identity[:])
         zeros = keep.tile([2, D_IN], F32)
         nc.vector.memset(zeros[:], 0.0)
+        idle_in = keep.tile([P, N_TILE], BF16)
+        nc.gpsimd.memset(idle_in[:], 0.0)
 
         w_raw = keep.tile([P, PASSES, PACK, D_IN], BF16)
         w_view = W_r.rearrange("(g u p e) n -> g p u (e n)", g=PASSES, u=2, p=P, e=2)
@@ -157,6 +160,9 @@ def tile_relativemultiheadattention_pa_kernel(tc, pos_embed, W_r, b_r, grad_out,
                 quantise_w(g, n)
             if g == 0:
                 transpose_tiles(0, 1)
+                idle_out = sums.tile([P, N_TILE], F32, tag="acc")
+                for i in range(WARM):
+                    nc.tensor.matmul(idle_out[:], lhsT=idle_in[:, 0:P], rhs=idle_in[:], start=True, stop=True)
                 regroup_tile(0)
                 quantise_tile(0)
         transpose_tiles(1, RUN)

@@ -20,6 +20,7 @@ N_TILES = D_IN // N_TILE
 RUN = 3
 AHEAD = 2
 PSUM_BANKS = 8
+V_COLS = 320
 WARM = 6
 
 FLOPS = 2 * ROWS * D_OUT * D_IN
@@ -86,10 +87,9 @@ def tile_relativemultiheadattention_pa_kernel(tc, pos_embed, W_r, b_r, grad_out,
         w_scales = keep.tile([P, PASSES, D_IN], U8, align_bytes=64)
 
         def regroup_w(g, n):
-            half = N_TILE // 2
-            shares = ((nc.vector.tensor_copy, n * N_TILE), (nc.scalar.copy, n * N_TILE + half))
-            for copy, first in shares:
-                cols = slice(first, first + half)
+            shares = ((nc.vector.tensor_copy, n * N_TILE, V_COLS), (nc.scalar.copy, n * N_TILE + V_COLS, N_TILE - V_COLS))
+            for copy, first, width in shares:
+                cols = slice(first, first + width)
                 copy(
                     out=w_grouped[:, g, cols, :].rearrange("p (c i) t -> p c t i", i=4),
                     in_=w_raw[:, g, :, cols].rearrange("p t (c i) -> p c t i", i=4),

from contextlib import ExitStack

import concourse.mybir as mybir
from concourse.masks import make_identity

BF16 = mybir.dt.bfloat16
F32 = mybir.dt.float32
U32 = mybir.dt.uint32
U8 = mybir.dt.uint8
E4M3_X4 = mybir.dt.float8_e4m3fn_x4
E5M2_X4 = mybir.dt.float8_e5m2_x4

BATCH, SEQ, D_IN, D_OUT = 3, 512, 1024, 1024
ROWS = BATCH * SEQ
P = 128
PACK = 4
PASSES = D_OUT // (P * PACK)
N_TILE = 512
N_TILES = D_IN // N_TILE
RUN = 3
AHEAD = 2
PSUM_BANKS = 8
V_COLS = 320
WARM = 6

FLOPS = 2 * ROWS * D_OUT * D_IN
BYTES = 2 * ROWS * D_OUT + 2 * D_OUT * D_IN + 4 * ROWS * D_IN


def row_tiles():
    tiles = []
    for b in range(BATCH):
        first_s = 2 if b == 0 else 0
        for s in range(first_s, SEQ, P):
            tiles.append(((SEQ + 1) * b + s - 2, SEQ * b + s, min(P, SEQ - s)))
    return tiles


def tile_relativemultiheadattention_pa_kernel(tc, pos_embed, W_r, b_r, grad_out, out):
    nc = tc.nc
    grad_rows = grad_out.flatten_outer_dims()
    out_rows = out.flatten_outer_dims()
    tiles = row_tiles()
    n_tiles = len(tiles)
    assert n_tiles % RUN == 0 and AHEAD <= RUN

    with ExitStack() as ctx:
        keep = ctx.enter_context(tc.tile_pool(name="keep", bufs=1))
        per_tile = ctx.enter_context(tc.tile_pool(name="per_tile", bufs=n_tiles))
        transposed = ctx.enter_context(tc.psum_pool(name="transposed", bufs=RUN))
        sums = ctx.enter_context(tc.psum_pool(name="sums", bufs=PSUM_BANKS - RUN))
        ctx.enter_context(tc.manual_schedule())

        identity = keep.tile([P, P], F32)
        make_identity(nc, identity[:])
        zeros = keep.tile([2, D_IN], F32)
        nc.vector.memset(zeros[:], 0.0)
        idle_in = keep.tile([P, N_TILE], BF16)
        nc.gpsimd.memset(idle_in[:], 0.0)

        w_raw = keep.tile([P, PASSES, PACK, D_IN], BF16)
        w_view = W_r.rearrange("(g u p e) n -> g p u (e n)", g=PASSES, u=2, p=P, e=2)

        def load_w(g):
            nc.sync.dma_start(out=w_raw[:, g].rearrange("p (u e) n -> p u (e n)", u=2), in_=w_view[g])

        raw_tiles = {}

        def load_tile(j):
            first_g, first_o, rows = tiles[j]
            raw = per_tile.tile([P, D_OUT], BF16)
            nc.sync.dma_start(out=raw[0:rows, :], in_=grad_rows[first_g : first_g + rows, :])
            if rows < P:
                assert P - rows == BATCH - 1
                nc.sync.dma_start(out=raw[rows:P, :], in_=grad_rows[SEQ - 2 : ROWS - SEQ : SEQ + 1, :])
            raw_tiles[j] = raw

        load_w(0)
        load_tile(0)
        load_w(1)
        for j in range(1, n_tiles):
            load_tile(j)
        nc.sync.dma_start(out=out_rows[0:2, :], in_=zeros[:])

        w_grouped = keep.tile([P, PASSES, D_IN, PACK], BF16, align_bytes=64)
        w_codes = keep.tile([P, PASSES, D_IN], U32, align_bytes=64)
        w_scales = keep.tile([P, PASSES, D_IN], U8, align_bytes=64)

        def regroup_w(g, n):
            shares = ((nc.vector.tensor_copy, n * N_TILE, V_COLS), (nc.scalar.copy, n * N_TILE + V_COLS, N_TILE - V_COLS))
            for copy, first, width in shares:
                cols = slice(first, first + width)
                copy(
                    out=w_grouped[:, g, cols, :].rearrange("p (c i) t -> p c t i", i=4),
                    in_=w_raw[:, g, :, cols].rearrange("p t (c i) -> p c t i", i=4),
                )

        def quantise_w(g, n):
            cols = slice(n * N_TILE, (n + 1) * N_TILE)
            nc.vector.quantize_mx(
                out=w_codes[:, g, cols].bitcast(E4M3_X4),
                scales=w_scales[:, g, cols],
                in_=w_grouped[:, g, cols, :].rearrange("p c t -> p (c t)"),
            )

        g_codes = keep.tile([P, n_tiles, PASSES, P], U32, align_bytes=64)
        g_scales = keep.tile([P, n_tiles, PASSES, P], U8, align_bytes=64)
        banks = {}
        grouped_tiles = {}

        def transpose_tiles(first, end):
            for j in range(first, end):
                words = raw_tiles[j][:].bitcast(F32)
                bank = transposed.tile([P, PASSES * 2, P], F32)
                for c in range(PASSES * 2):
                    nc.tensor.transpose(bank[:, c, :], words[:, c * P : (c + 1) * P], identity[:])
                banks[j] = bank

        def regroup_tile(j):
            grouped = per_tile.tile([P, PASSES * P * PACK], BF16, align_bytes=64)
            nc.scalar.copy(
                out=grouped[:].bitcast(F32).rearrange("p (g r u) -> p g r u", g=PASSES, u=2),
                in_=banks[j][:].rearrange("p (g u) r -> p g r u", u=2),
            )
            grouped_tiles[j] = grouped

        def quantise_tile(j):
            nc.vector.quantize_mx(
                out=g_codes[:, j].rearrange("p g r -> p (g r)").bitcast(E5M2_X4),
                scales=g_scales[:, j].rearrange("p g r -> p (g r)"),
                in_=grouped_tiles[j][:],
            )

        def multiply_tile(j):
            first_g, first_o, rows = tiles[j]
            result = per_tile.tile([P, D_IN], F32)
            for n in range(N_TILES):
                cols = slice(n * N_TILE, (n + 1) * N_TILE)
                acc = sums.tile([P, N_TILE], F32)
                for g in range(PASSES):
                    nc.tensor.matmul_mx(
                        out=acc[:],
                        lhsT=g_codes[:, j, g, :].bitcast(E5M2_X4),
                        lhsT_scale=g_scales[:, j, g, :],
                        rhs=w_codes[:, g, cols].bitcast(E4M3_X4),
                        rhs_scale=w_scales[:, g, cols],
                        start=(g == 0),
                        stop=(g == PASSES - 1),
                    )
                if n % 2 == 0:
                    nc.vector.tensor_copy(out=result[:, cols], in_=acc[:])
                else:
                    nc.scalar.copy(out=result[:, cols], in_=acc[:])
                nc.sync.dma_start(out=out_rows[first_o : first_o + rows, cols], in_=result[0:rows, cols])

        for g in range(PASSES):
            for n in range(N_TILES):
                regroup_w(g, n)
            for n in range(N_TILES):
                quantise_w(g, n)
            if g == 0:
                transpose_tiles(0, 1)
                idle_out = sums.tile([P, N_TILE], F32, tag="acc")
                for i in range(WARM):
                    nc.tensor.matmul(idle_out[:], lhsT=idle_in[:, 0:P], rhs=idle_in[:], start=True, stop=True)
                regroup_tile(0)
                quantise_tile(0)
        transpose_tiles(1, RUN)
        for j in range(1, AHEAD):
            regroup_tile(j)
            quantise_tile(j)
        for j in range(n_tiles):
            ahead = j + AHEAD
            if ahead < n_tiles:
                if ahead % RUN == 0:
                    transpose_tiles(ahead, ahead + RUN)
                regroup_tile(ahead)
            multiply_tile(j)
            if ahead < n_tiles:
                quantise_tile(ahead)
